import numpy as np
import ml_dtypes


def mxq(x, axis, fmt="e4m3"):
    dtype, down = {"e4m3": (ml_dtypes.float8_e4m3fn, 7), "e5m2": (ml_dtypes.float8_e5m2, 14)}[fmt]
    v = np.moveaxis(np.asarray(x, np.float32).astype(ml_dtypes.bfloat16).astype(np.float64), axis, -1)
    blocks = v.reshape(v.shape[:-1] + (-1, 32))
    amax = np.abs(blocks).max(-1, keepdims=True)
    byte = np.maximum(np.where(amax > 0, np.frexp(amax)[1] - 1 + 127, 0) - down, 1)
    scale = np.exp2(byte - 127.0)
    codes = (blocks / scale).astype(np.float32).astype(dtype).astype(np.float64)
    return np.moveaxis((codes * scale).reshape(v.shape), -1, axis)


WIDE = False


def mx_kscale(k):
    if not WIDE:
        return np.ones(k)
    levels = np.array([10, -10, 5, -5, 0])
    a = np.random.permutation(np.resize(levels, k // 512 * 4)).reshape(k // 512, 4)
    idx = np.arange(k)
    return np.exp2(a[idx // 512, idx % 128 // 32])


BF16 = ml_dtypes.bfloat16


def bf(x):
    return np.asarray(x, np.float32).astype(BF16)


def f64(x):
    return np.asarray(x).astype(np.float64)


E2M1 = np.array([0.0, 0.5, 1.0, 1.5, 2.0, 3.0, 4.0, 6.0, -0.0, -0.5, -1.0, -1.5, -2.0, -3.0, -4.0, -6.0])


def pack_weight(w, fmt):
    k, n = w.shape
    w = f64(bf(w)).reshape(k // 32, 32, n)
    amax = np.abs(w).max(1)
    if fmt == "e4m3":
        byte = np.frexp(amax)[1] - 1 + 127 - 7
    else:
        mant, ex = np.frexp(amax / 6.0)
        byte = np.where(mant > 0.5, ex, ex - 1) + 127
    byte = np.clip(np.where(amax > 0, byte, 1), 1, 254)
    scaled = (w * np.exp2(127.0 - byte)[:, None, :]).reshape(k, n).astype(np.float32)
    by_word = np.ascontiguousarray(scaled.reshape(k // 512, 128, 4, n).transpose(0, 1, 3, 2))
    if fmt == "e4m3":
        words = by_word.astype(ml_dtypes.float8_e4m3fn).view(np.uint8)
    else:
        c = by_word.astype(ml_dtypes.float4_e2m1fn).view(np.uint8) & 0xF
        words = c[..., 0::2] | (c[..., 1::2] << 4)
    return np.ascontiguousarray(words), np.ascontiguousarray(byte.astype(np.uint8).reshape(k // 512, 16, n))


def unpack_weight(words, scales, fmt):
    g, p, n, _ = words.shape
    if fmt == "e4m3":
        vals = np.ascontiguousarray(words).view(ml_dtypes.float8_e4m3fn).astype(np.float64)
    else:
        nib = np.empty((g, p, n, 4), np.uint8)
        nib[..., 0::2] = words & 0xF
        nib[..., 1::2] = words >> 4
        vals = E2M1[nib]
    vals = vals * np.repeat(np.exp2(scales.astype(np.float64) - 127.0), 8, axis=1)[..., None]
    return vals.transpose(0, 1, 3, 2).reshape(g * 512, n)

def pack4(w):
    words, scales = pack_weight(w, "e2m1")
    return words.reshape(words.shape[0], 128, -1), scales


def unpack4(words, scales):
    return unpack_weight(words.reshape(words.shape[0], 128, -1, 2), scales, "e2m1")


N, MUL, RANK, D0, D1, D2 = 1024, 512, 128, 1, 3, 5
DIMS = (D0, D1, D2)
SD = D0 + D1 + D2
NI = len(DIMS)
SCALING = 2.0


def setup_inputs():
    s = mx_kscale(MUL)
    x = bf(np.random.standard_normal((N, SD * MUL)) * np.tile(s, SD))
    a_lora = bf(np.random.standard_normal((N, SD * RANK)) * 0.5)
    stack = np.random.standard_normal((NI, MUL, MUL)) / s[None, :, None]
    words, scales = pack4(stack.reshape(-1, MUL))
    w_lora_b = bf(np.random.standard_normal((NI, RANK, MUL)))
    return {"x": x,
            "a_lora": a_lora,
            "w_base_words": words,
            "w_base_scales": scales,
            "w_lora_b": w_lora_b}


def reference(x, a_lora, w_base_words, w_base_scales, w_lora_b):
    x, a_lora, w_lora_b = f64(x), f64(a_lora), f64(w_lora_b)
    w_base = unpack4(w_base_words, w_base_scales).reshape(NI, MUL, MUL)
    pw_base = 1.0 / np.sqrt(MUL)
    pw_b = 1.0 / np.sqrt(RANK)
    n = x.shape[0]
    outs = []
    off = 0
    offa = 0
    for k, d in enumerate(DIMS):
        seg = x[:, off:off + d * MUL].reshape(n * d, MUL)
        y = pw_base * (mxq(seg, 1, "e4m3") @ w_base[k])
        a = a_lora[:, offa:offa + d * RANK].reshape(n * d, RANK)
        b = pw_b * (a @ w_lora_b[k])
        outs.append((y + SCALING * b).reshape(n, d * MUL))
        off += d * MUL
        offa += d * RANK
    return np.concatenate(outs, axis=-1)

@@ -1,0 +1,196 @@
+import math
+from contextlib import ExitStack
+
+import concourse.mybir as mybir
+from concourse.masks import make_identity
+
+BF16 = mybir.dt.bfloat16
+F32 = mybir.dt.float32
+I32 = mybir.dt.int32
+U8 = mybir.dt.uint8
+U32 = mybir.dt.uint32
+FP8X4 = mybir.dt.float8_e4m3fn_x4
+FP4X4 = mybir.dt.float4_e2m1fn_x4
+
+P = 128
+PACK = 4
+NODES = 1024
+MUL = 512
+RANK = 128
+IRREP_DIMS = (1, 3, 5)
+IRREPS = len(IRREP_DIMS)
+IRREP_OF_BLOCK = tuple(k for k, d in enumerate(IRREP_DIMS) for c in range(d))
+BLOCKS = len(IRREP_OF_BLOCK)
+NODES_PER_PARTITION = NODES // P
+
+PANELS = NODES_PER_PARTITION * BLOCKS
+STEP = 2
+STEPS = PANELS // STEP
+AHEAD = 2
+LOAD = 8
+STORE = 4
+
+BASE_FACTOR = 1.0 / math.sqrt(MUL)
+LORA_FACTOR = 2.0 / math.sqrt(RANK)
+
+FLOPS = 2 * NODES * BLOCKS * MUL * (MUL + RANK)
+
+
+def tile_loracuetlinear_pa_t_e_kernel(tc, x, a_lora, w_base_words, w_base_scales, w_lora_b, out):
+    nc = tc.nc
+    x_panels = x.rearrange("(p t) c -> p (t c)", p=P).rearrange("p (m k) -> p m k", k=MUL)
+    a_panels = a_lora.rearrange("(p t) c -> p (t c)", p=P).rearrange("p (m r) -> p m r", r=RANK)
+    out_panels = out.rearrange("(p t) c -> p (t c)", p=P).rearrange("p (m c) -> p m c", c=MUL)
+
+    with ExitStack() as ctx:
+        keep = ctx.enter_context(tc.tile_pool(name="keep", bufs=1))
+        ring = ctx.enter_context(tc.tile_pool(name="ring", bufs=4))
+        results = ctx.enter_context(tc.tile_pool(name="results", bufs=8))
+        psum = ctx.enter_context(tc.psum_pool(name="psum", bufs=2))
+        ctx.enter_context(tc.manual_schedule())
+
+        ident_f32 = keep.tile([P, P], F32)
+        make_identity(nc, ident_f32[:])
+        ident_bf16 = keep.tile([P, P], BF16)
+        make_identity(nc, ident_bf16[:])
+
+        w_words = keep.tile([P, IRREPS, 2 * MUL], U8, align_bytes=64)
+        w_planes = keep.tile([P, IRREPS, MUL], U8, align_bytes=64)
+        nc.vector.memset(w_planes[:].bitcast(I32), 0)
+        w_lora = keep.tile([P, IRREPS, MUL], BF16)
+
+        x_loads = []
+        a_loads = []
+        for c in range(PANELS // LOAD):
+            panels = slice(c * LOAD, (c + 1) * LOAD)
+            x_load = keep.tile([P, LOAD, MUL], BF16, name="x_load%d" % c)
+            nc.sync.dma_start(out=x_load[:], in_=x_panels[:, panels, :])
+            x_loads.append(x_load)
+            a_load = keep.tile([P, LOAD, RANK], BF16, name="a_load%d" % c)
+            nc.sync.dma_start(out=a_load[:], in_=a_panels[:, panels, :])
+            a_loads.append(a_load)
+            if c == 0:
+                nc.sync.dma_start(out=w_lora[:], in_=w_lora_b.rearrange("g r c -> r g c"))
+                nc.sync.dma_start(
+                    out=w_words[:].bitcast(I32), in_=w_base_words.bitcast(I32).rearrange("g p w -> p g w")
+                )
+                for quadrant in range(4):
+                    nc.sync.dma_start(
+                        out=w_planes[32 * quadrant : 32 * quadrant + 4, :, :].bitcast(I32),
+                        in_=w_base_scales.bitcast(I32)[:, 4 * quadrant : 4 * quadrant + 4, :].rearrange(
+                            "g q w -> q g w"
+                        ),
+                    )
+
+        xT_banks = {}
+        aT_banks = {}
+        grouped_tiles = {}
+        aT_tiles = {}
+        code_tiles = {}
+        plane_tiles = {}
+        lora_banks = {}
+        mx_banks = {}
+        lora_tiles = {}
+        out_tiles = {}
+
+        def transpose_panel(s, i):
+            m = STEP * s + i
+            if i == 0:
+                xT_banks[s] = psum.tile([P, STEP, 2, P], F32, name="xT_bank")
+                aT_banks[s] = psum.tile([P, STEP, P], BF16, name="aT_bank")
+            x_words = x_loads[m // LOAD][:, m % LOAD, :].bitcast(F32)
+            for u in range(2):
+                nc.tensor.transpose(xT_banks[s][:, i, u, :], x_words[:, u : MUL // 2 : 2], ident_f32[:])
+            nc.tensor.transpose(aT_banks[s][:, i, :], a_loads[m // LOAD][:, m % LOAD, :], ident_bf16[:])
+
+        def copy_x_out(s):
+            grouped = ring.tile([P, STEP, P, PACK], BF16, name="grouped", align_bytes=64)
+            nc.scalar.copy(out=grouped[:].bitcast(F32), in_=xT_banks[s][:].rearrange("p i u n -> p i n u"))
+            grouped_tiles[s] = grouped
+
+        def copy_a_out(s):
+            aT = ring.tile([P, STEP, P], BF16, name="aT")
+            nc.vector.tensor_copy(out=aT[:], in_=aT_banks[s][:])
+            aT_tiles[s] = aT
+
+        def quantise(s):
+            codes = ring.tile([P, STEP * P], U32, name="codes", align_bytes=64)
+            planes = ring.tile([P, STEP * P], U8, name="planes", align_bytes=64)
+            nc.vector.quantize_mx(
+                out=codes[:].bitcast(FP8X4),
+                scales=planes[:],
+                in_=grouped_tiles[s][:].rearrange("p i n t -> p (i n t)"),
+            )
+            code_tiles[s] = codes
+            plane_tiles[s] = planes
+
+        def lora_product(s, i):
+            m = STEP * s + i
+            g = IRREP_OF_BLOCK[m % BLOCKS]
+            lora_banks[m] = psum.tile([P, MUL], F32, name="lora_bank")
+            nc.tensor.matmul(lora_banks[m][:], lhsT=aT_tiles[s][:, i, :], rhs=w_lora[:, g, :], start=True, stop=True)
+
+        def base_product(s, i):
+            m = STEP * s + i
+            g = IRREP_OF_BLOCK[m % BLOCKS]
+            nodes = slice(i * P, (i + 1) * P)
+            mx_banks[m] = psum.tile([P, MUL], F32, name="mx_bank")
+            nc.tensor.matmul_mx(
+                out=mx_banks[m][:],
+                lhsT=code_tiles[s][:, nodes].bitcast(FP8X4),
+                lhsT_scale=plane_tiles[s][:, nodes],
+                rhs=w_words[:, g, :].bitcast(FP4X4),
+                rhs_scale=w_planes[:, g, :],
+                start=True,
+                stop=True,
+            )
+
+        def scale_lora(m):
+            lora_tiles[m] = ring.tile([P, MUL], F32, name="lora_scaled")
+            nc.scalar.activation(
+                out=lora_tiles[m][:], in_=lora_banks[m][:], func=mybir.ActivationFunctionType.Copy, scale=LORA_FACTOR
+            )
+
+        def combine_and_store(m):
+            group = m // STORE
+            if m % STORE == 0:
+                out_tiles[group] = results.tile([P, STORE, MUL], F32, name="out_tile")
+            nc.vector.scalar_tensor_tensor(
+                out=out_tiles[group][:, m % STORE, :],
+                in0=mx_banks[m][:],
+                scalar=BASE_FACTOR,
+                in1=lora_tiles[m][:],
+                op0=mybir.AluOpType.mult,
+                op1=mybir.AluOpType.add,
+            )
+            if m % STORE == STORE - 1:
+                nc.sync.dma_start(
+                    out=out_panels[:, group * STORE : (group + 1) * STORE, :], in_=out_tiles[group][:]
+                )
+
+        for s in range(AHEAD):
+            for i in range(STEP):
+                transpose_panel(s, i)
+            copy_x_out(s)
+            copy_a_out(s)
+        for s in range(AHEAD - 1):
+            quantise(s)
+
+        for s in range(STEPS):
+            ahead = s + AHEAD
+            for i in range(STEP):
+                lora_product(s, i)
+                if ahead < STEPS:
+                    transpose_panel(ahead, i)
+            for i in range(STEP):
+                base_product(s, i)
+            for i in range(STEP):
+                scale_lora(STEP * s + i)
+            if ahead < STEPS:
+                copy_x_out(ahead)
+            if ahead - 1 < STEPS:
+                quantise(ahead - 1)
+            if ahead < STEPS:
+                copy_a_out(ahead)
+            for i in range(STEP):
+                combine_and_store(STEP * s + i)

@@ -28,6 +28,7 @@ STEP = 2
 STEPS = PANELS // STEP
 AHEAD = 2
 LOAD = 8
+FIRST_LOAD = STEP * AHEAD
 STORE = 4
 
 BASE_FACTOR = 1.0 / math.sqrt(MUL)
@@ -59,28 +60,32 @@ def tile_loracuetlinear_pa_t_e_kernel(tc, x, a_lora, w_base_words, w_base_scales
         nc.vector.memset(w_planes[:].bitcast(I32), 0)
         w_lora = keep.tile([P, IRREPS, MUL], BF16)
 
-        x_loads = []
-        a_loads = []
-        for c in range(PANELS // LOAD):
-            panels = slice(c * LOAD, (c + 1) * LOAD)
-            x_load = keep.tile([P, LOAD, MUL], BF16, name="x_load%d" % c)
-            nc.sync.dma_start(out=x_load[:], in_=x_panels[:, panels, :])
-            x_loads.append(x_load)
-            a_load = keep.tile([P, LOAD, RANK], BF16, name="a_load%d" % c)
-            nc.sync.dma_start(out=a_load[:], in_=a_panels[:, panels, :])
-            a_loads.append(a_load)
-            if c == 0:
-                nc.sync.dma_start(out=w_lora[:], in_=w_lora_b.rearrange("g r c -> r g c"))
+        x_of_panel = {}
+        a_of_panel = {}
+
+        def load_panels(source, width, first, count, name, of_panel):
+            loaded = keep.tile([P, count, width], BF16, name="%s%d" % (name, first))
+            nc.sync.dma_start(out=loaded[:], in_=source[:, first : first + count, :])
+            for i in range(count):
+                of_panel[first + i] = loaded[:, i, :]
+
+        def load_weights():
+            nc.sync.dma_start(out=w_lora[:], in_=w_lora_b.rearrange("g r c -> r g c"))
+            nc.sync.dma_start(out=w_words[:].bitcast(I32), in_=w_base_words.bitcast(I32).rearrange("g p w -> p g w"))
+            for quadrant in range(4):
                 nc.sync.dma_start(
-                    out=w_words[:].bitcast(I32), in_=w_base_words.bitcast(I32).rearrange("g p w -> p g w")
+                    out=w_planes[32 * quadrant : 32 * quadrant + 4, :, :].bitcast(I32),
+                    in_=w_base_scales.bitcast(I32)[:, 4 * quadrant : 4 * quadrant + 4, :].rearrange("g q w -> q g w"),
                 )
-                for quadrant in range(4):
-                    nc.sync.dma_start(
-                        out=w_planes[32 * quadrant : 32 * quadrant + 4, :, :].bitcast(I32),
-                        in_=w_base_scales.bitcast(I32)[:, 4 * quadrant : 4 * quadrant + 4, :].rearrange(
-                            "g q w -> q g w"
-                        ),
-                    )
+
+        load_panels(x_panels, MUL, 0, FIRST_LOAD, "x_load", x_of_panel)
+        load_panels(a_panels, RANK, 0, LOAD, "a_load", a_of_panel)
+        load_weights()
+        for first in range(FIRST_LOAD, LOAD, FIRST_LOAD):
+            load_panels(x_panels, MUL, first, FIRST_LOAD, "x_load", x_of_panel)
+        for first in range(LOAD, PANELS, LOAD):
+            load_panels(x_panels, MUL, first, LOAD, "x_load", x_of_panel)
+            load_panels(a_panels, RANK, first, LOAD, "a_load", a_of_panel)
 
         xT_banks = {}
         aT_banks = {}
@@ -98,10 +103,10 @@ def tile_loracuetlinear_pa_t_e_kernel(tc, x, a_lora, w_base_words, w_base_scales
             if i == 0:
                 xT_banks[s] = psum.tile([P, STEP, 2, P], F32, name="xT_bank")
                 aT_banks[s] = psum.tile([P, STEP, P], BF16, name="aT_bank")
-            x_words = x_loads[m // LOAD][:, m % LOAD, :].bitcast(F32)
+            x_words = x_of_panel[m].bitcast(F32)
             for u in range(2):
                 nc.tensor.transpose(xT_banks[s][:, i, u, :], x_words[:, u : MUL // 2 : 2], ident_f32[:])
-            nc.tensor.transpose(aT_banks[s][:, i, :], a_loads[m // LOAD][:, m % LOAD, :], ident_bf16[:])
+            nc.tensor.transpose(aT_banks[s][:, i, :], a_of_panel[m], ident_bf16[:])
 
         def copy_x_out(s):
             grouped = ring.tile([P, STEP, P, PACK], BF16, name="grouped", align_bytes=64)
@@ -163,7 +168,9 @@ def tile_loracuetlinear_pa_t_e_kernel(tc, x, a_lora, w_base_words, w_base_scales
                 op0=mybir.AluOpType.mult,
                 op1=mybir.AluOpType.add,
             )
-            if m % STORE == STORE - 1:
+            if m >= PANELS - STORE:
+                nc.sync.dma_start(out=out_panels[:, m, :], in_=out_tiles[group][:, m % STORE, :])
+            elif m % STORE == STORE - 1:
                 nc.sync.dma_start(
                     out=out_panels[:, group * STORE : (group + 1) * STORE, :], in_=out_tiles[group][:]
                 )

@@ -27,9 +27,8 @@ PANELS = NODES_PER_PARTITION * BLOCKS
 STEP = 2
 STEPS = PANELS // STEP
 AHEAD = 2
-LOAD = 8
-FIRST_LOAD = STEP * AHEAD
-STORE = 4
+FIRST_LOAD = 8
+STORE = 8
 
 BASE_FACTOR = 1.0 / math.sqrt(MUL)
 LORA_FACTOR = 2.0 / math.sqrt(RANK)
@@ -46,7 +45,7 @@ def tile_loracuetlinear_pa_t_e_kernel(tc, x, a_lora, w_base_words, w_base_scales
     with ExitStack() as ctx:
         keep = ctx.enter_context(tc.tile_pool(name="keep", bufs=1))
         ring = ctx.enter_context(tc.tile_pool(name="ring", bufs=4))
-        results = ctx.enter_context(tc.tile_pool(name="results", bufs=8))
+        results = ctx.enter_context(tc.tile_pool(name="results", bufs=6))
         psum = ctx.enter_context(tc.psum_pool(name="psum", bufs=2))
         ctx.enter_context(tc.manual_schedule())
 
@@ -62,30 +61,35 @@ def tile_loracuetlinear_pa_t_e_kernel(tc, x, a_lora, w_base_words, w_base_scales
 
         x_of_panel = {}
         a_of_panel = {}
-
-        def load_panels(source, width, first, count, name, of_panel):
-            loaded = keep.tile([P, count, width], BF16, name="%s%d" % (name, first))
-            nc.sync.dma_start(out=loaded[:], in_=source[:, first : first + count, :])
+        first = 0
+        count = FIRST_LOAD
+        while first < PANELS:
+            x_load = keep.tile([P, count, MUL], BF16, name="x_load%d" % first)
+            nc.sync.dma_start(out=x_load[:], in_=x_panels[:, first : first + count, :])
+            a_load = keep.tile([P, count, RANK], BF16, name="a_load%d" % first)
+            nc.sync.dma_start(out=a_load[:], in_=a_panels[:, first : first + count, :])
             for i in range(count):
-                of_panel[first + i] = loaded[:, i, :]
-
-        def load_weights():
-            nc.sync.dma_start(out=w_lora[:], in_=w_lora_b.rearrange("g r c -> r g c"))
-            nc.sync.dma_start(out=w_words[:].bitcast(I32), in_=w_base_words.bitcast(I32).rearrange("g p w -> p g w"))
-            for quadrant in range(4):
+                x_of_panel[first + i] = x_load[:, i, :]
+                a_of_panel[first + i] = a_load[:, i, :]
+            if first == 0:
+                nc.sync.dma_start(out=w_lora[:], in_=w_lora_b.rearrange("g r c -> r g c"))
                 nc.sync.dma_start(
-                    out=w_planes[32 * quadrant : 32 * quadrant + 4, :, :].bitcast(I32),
-                    in_=w_base_scales.bitcast(I32)[:, 4 * quadrant : 4 * quadrant + 4, :].rearrange("g q w -> q g w"),
+                    out=w_words[:].bitcast(I32), in_=w_base_words.bitcast(I32).rearrange("g p w -> p g w")
                 )
+                for quadrant in range(4):
+                    nc.sync.dma_start(
+                        out=w_planes[32 * quadrant : 32 * quadrant + 4, :, :].bitcast(I32),
+                        in_=w_base_scales.bitcast(I32)[:, 4 * quadrant : 4 * quadrant + 4, :].rearrange(
+                            "g q w -> q g w"
+                        ),
+                    )
+            first += count
+            count = min(first, PANELS - first)
 
-        load_panels(x_panels, MUL, 0, FIRST_LOAD, "x_load", x_of_panel)
-        load_panels(a_panels, RANK, 0, LOAD, "a_load", a_of_panel)
-        load_weights()
-        for first in range(FIRST_LOAD, LOAD, FIRST_LOAD):
-            load_panels(x_panels, MUL, first, FIRST_LOAD, "x_load", x_of_panel)
-        for first in range(LOAD, PANELS, LOAD):
-            load_panels(x_panels, MUL, first, LOAD, "x_load", x_of_panel)
-            load_panels(a_panels, RANK, first, LOAD, "a_load", a_of_panel)
+        store_starts = list(range(0, PANELS, STORE))
+        while PANELS - store_starts[-1] > STEP:
+            store_starts.append((store_starts[-1] + PANELS) // 2)
+        store_ends = store_starts[1:] + [PANELS]
 
         xT_banks = {}
         aT_banks = {}
@@ -157,23 +161,21 @@ def tile_loracuetlinear_pa_t_e_kernel(tc, x, a_lora, w_base_words, w_base_scales
             )
 
         def combine_and_store(m):
-            group = m // STORE
-            if m % STORE == 0:
-                out_tiles[group] = results.tile([P, STORE, MUL], F32, name="out_tile")
+            group = max(g for g in range(len(store_starts)) if store_starts[g] <= m)
+            start = store_starts[group]
+            end = store_ends[group]
+            if m == start:
+                out_tiles[group] = results.tile([P, end - start, MUL], F32, name="out_tile")
             nc.vector.scalar_tensor_tensor(
-                out=out_tiles[group][:, m % STORE, :],
+                out=out_tiles[group][:, m - start, :],
                 in0=mx_banks[m][:],
                 scalar=BASE_FACTOR,
                 in1=lora_tiles[m][:],
                 op0=mybir.AluOpType.mult,
                 op1=mybir.AluOpType.add,
             )
-            if m >= PANELS - STORE:
-                nc.sync.dma_start(out=out_panels[:, m, :], in_=out_tiles[group][:, m % STORE, :])
-            elif m % STORE == STORE - 1:
-                nc.sync.dma_start(
-                    out=out_panels[:, group * STORE : (group + 1) * STORE, :], in_=out_tiles[group][:]
-                )
+            if m == end - 1:
+                nc.sync.dma_start(out=out_panels[:, start:end, :], in_=out_tiles[group][:])
 
         for s in range(AHEAD):
             for i in range(STEP):

@@ -26,9 +26,11 @@ NODES_PER_PARTITION = NODES // P
 PANELS = NODES_PER_PARTITION * BLOCKS
 STEP = 2
 STEPS = PANELS // STEP
-AHEAD = 2
-FIRST_LOAD = 8
-STORE = 8
+AHEAD = 3
+LOADS = (2, 2, 4, 4, 8, 16, 36)
+LOADS_BEFORE_WEIGHTS = 3
+WARM_UP = 5
+STORES = (8, 8, 8, 8, 8, 8, 8, 6, 4, 3, 2, 1)
 
 BASE_FACTOR = 1.0 / math.sqrt(MUL)
 LORA_FACTOR = 2.0 / math.sqrt(RANK)
@@ -49,6 +51,8 @@ def tile_loracuetlinear_pa_t_e_kernel(tc, x, a_lora, w_base_words, w_base_scales
         psum = ctx.enter_context(tc.psum_pool(name="psum", bufs=2))
         ctx.enter_context(tc.manual_schedule())
 
+        zeros = keep.tile([P, MUL], BF16)
+        nc.vector.memset(zeros[:], 0.0)
         ident_f32 = keep.tile([P, P], F32)
         make_identity(nc, ident_f32[:])
         ident_bf16 = keep.tile([P, P], BF16)
@@ -62,8 +66,7 @@ def tile_loracuetlinear_pa_t_e_kernel(tc, x, a_lora, w_base_words, w_base_scales
         x_of_panel = {}
         a_of_panel = {}
         first = 0
-        count = FIRST_LOAD
-        while first < PANELS:
+        for number, count in enumerate(LOADS):
             x_load = keep.tile([P, count, MUL], BF16, name="x_load%d" % first)
             nc.sync.dma_start(out=x_load[:], in_=x_panels[:, first : first + count, :])
             a_load = keep.tile([P, count, RANK], BF16, name="a_load%d" % first)
@@ -71,11 +74,7 @@ def tile_loracuetlinear_pa_t_e_kernel(tc, x, a_lora, w_base_words, w_base_scales
             for i in range(count):
                 x_of_panel[first + i] = x_load[:, i, :]
                 a_of_panel[first + i] = a_load[:, i, :]
-            if first == 0:
-                nc.sync.dma_start(out=w_lora[:], in_=w_lora_b.rearrange("g r c -> r g c"))
-                nc.sync.dma_start(
-                    out=w_words[:].bitcast(I32), in_=w_base_words.bitcast(I32).rearrange("g p w -> p g w")
-                )
+            if number == 0:
                 for quadrant in range(4):
                     nc.sync.dma_start(
                         out=w_planes[32 * quadrant : 32 * quadrant + 4, :, :].bitcast(I32),
@@ -83,13 +82,17 @@ def tile_loracuetlinear_pa_t_e_kernel(tc, x, a_lora, w_base_words, w_base_scales
                             "g q w -> q g w"
                         ),
                     )
+            if number == LOADS_BEFORE_WEIGHTS - 1:
+                nc.sync.dma_start(out=w_lora[:], in_=w_lora_b.rearrange("g r c -> r g c"))
+                nc.sync.dma_start(
+                    out=w_words[:].bitcast(I32), in_=w_base_words.bitcast(I32).rearrange("g p w -> p g w")
+                )
             first += count
-            count = min(first, PANELS - first)
+        assert first == PANELS
 
-        store_starts = list(range(0, PANELS, STORE))
-        while PANELS - store_starts[-1] > STEP:
-            store_starts.append((store_starts[-1] + PANELS) // 2)
+        store_starts = [sum(STORES[:g]) for g in range(len(STORES))]
         store_ends = store_starts[1:] + [PANELS]
+        assert sum(STORES) == PANELS
 
         xT_banks = {}
         aT_banks = {}
@@ -177,6 +180,9 @@ def tile_loracuetlinear_pa_t_e_kernel(tc, x, a_lora, w_base_words, w_base_scales
             if m == end - 1:
                 nc.sync.dma_start(out=out_panels[:, start:end, :], in_=out_tiles[group][:])
 
+        warm_bank = psum.tile([P, MUL], F32, name="lora_bank")
+        for w in range(WARM_UP):
+            nc.tensor.matmul(warm_bank[:], lhsT=zeros[:, :P], rhs=zeros[:], start=True, stop=True)
         for s in range(AHEAD):
             for i in range(STEP):
                 transpose_panel(s, i)

@@ -27,8 +27,22 @@ PANELS = NODES_PER_PARTITION * BLOCKS
 STEP = 2
 STEPS = PANELS // STEP
 AHEAD = 3
-LOADS = (2, 2, 4, 4, 8, 16, 36)
-LOADS_BEFORE_WEIGHTS = 3
+LOAD_ORDER = (
+    ("x", 2),
+    ("a", 8),
+    ("scales", 0),
+    ("x", 2),
+    ("x", 4),
+    ("weights", 0),
+    ("a", 8),
+    ("x", 4),
+    ("weights", 2),
+    ("x", 8),
+    ("a", 16),
+    ("x", 16),
+    ("a", 40),
+    ("x", 36),
+)
 WARM_UP = 5
 STORES = (8, 8, 8, 8, 8, 8, 8, 6, 4, 3, 2, 1)
 
@@ -51,8 +65,6 @@ def tile_loracuetlinear_pa_t_e_kernel(tc, x, a_lora, w_base_words, w_base_scales
         psum = ctx.enter_context(tc.psum_pool(name="psum", bufs=2))
         ctx.enter_context(tc.manual_schedule())
 
-        zeros = keep.tile([P, MUL], BF16)
-        nc.vector.memset(zeros[:], 0.0)
         ident_f32 = keep.tile([P, P], F32)
         make_identity(nc, ident_f32[:])
         ident_bf16 = keep.tile([P, P], BF16)
@@ -61,20 +73,26 @@ def tile_loracuetlinear_pa_t_e_kernel(tc, x, a_lora, w_base_words, w_base_scales
         w_words = keep.tile([P, IRREPS, 2 * MUL], U8, align_bytes=64)
         w_planes = keep.tile([P, IRREPS, MUL], U8, align_bytes=64)
         nc.vector.memset(w_planes[:].bitcast(I32), 0)
+        zeros = keep.tile([P, MUL], BF16)
+        nc.vector.memset(zeros[:], 0.0)
         w_lora = keep.tile([P, IRREPS, MUL], BF16)
 
         x_of_panel = {}
         a_of_panel = {}
-        first = 0
-        for number, count in enumerate(LOADS):
-            x_load = keep.tile([P, count, MUL], BF16, name="x_load%d" % first)
-            nc.sync.dma_start(out=x_load[:], in_=x_panels[:, first : first + count, :])
-            a_load = keep.tile([P, count, RANK], BF16, name="a_load%d" % first)
-            nc.sync.dma_start(out=a_load[:], in_=a_panels[:, first : first + count, :])
-            for i in range(count):
-                x_of_panel[first + i] = x_load[:, i, :]
-                a_of_panel[first + i] = a_load[:, i, :]
-            if number == 0:
+        for what, count in LOAD_ORDER:
+            if what == "x":
+                first = len(x_of_panel)
+                x_load = keep.tile([P, count, MUL], BF16, name="x_load%d" % first)
+                nc.sync.dma_start(out=x_load[:], in_=x_panels[:, first : first + count, :])
+                for i in range(count):
+                    x_of_panel[first + i] = x_load[:, i, :]
+            elif what == "a":
+                first = len(a_of_panel)
+                a_load = keep.tile([P, count, RANK], BF16, name="a_load%d" % first)
+                nc.sync.dma_start(out=a_load[:], in_=a_panels[:, first : first + count, :])
+                for i in range(count):
+                    a_of_panel[first + i] = a_load[:, i, :]
+            elif what == "scales":
                 for quadrant in range(4):
                     nc.sync.dma_start(
                         out=w_planes[32 * quadrant : 32 * quadrant + 4, :, :].bitcast(I32),
@@ -82,13 +100,14 @@ def tile_loracuetlinear_pa_t_e_kernel(tc, x, a_lora, w_base_words, w_base_scales
                             "g q w -> q g w"
                         ),
                     )
-            if number == LOADS_BEFORE_WEIGHTS - 1:
-                nc.sync.dma_start(out=w_lora[:], in_=w_lora_b.rearrange("g r c -> r g c"))
+            else:
+                irreps = slice(0, 2) if count == 0 else slice(2, IRREPS)
+                nc.sync.dma_start(out=w_lora[:, irreps, :], in_=w_lora_b[irreps].rearrange("g r c -> r g c"))
                 nc.sync.dma_start(
-                    out=w_words[:].bitcast(I32), in_=w_base_words.bitcast(I32).rearrange("g p w -> p g w")
+                    out=w_words[:, irreps, :].bitcast(I32),
+                    in_=w_base_words[irreps].bitcast(I32).rearrange("g p w -> p g w"),
                 )
-            first += count
-        assert first == PANELS
+        assert len(x_of_panel) == PANELS and len(a_of_panel) == PANELS
 
         store_starts = [sum(STORES[:g]) for g in range(len(STORES))]
         store_ends = store_starts[1:] + [PANELS]

@@ -128,7 +128,7 @@ def tile_loracuetlinear_pa_t_e_kernel(tc, x, a_lora, w_base_words, w_base_scales
             m = STEP * s + i
             if i == 0:
                 xT_banks[s] = psum.tile([P, STEP, 2, P], F32, name="xT_bank")
-                aT_banks[s] = psum.tile([P, STEP, P], BF16, name="aT_bank")
+                aT_banks[s] = psum.tile([P, STEP, P], BF16, name="aT_bank", bufs=1)
             x_words = x_of_panel[m].bitcast(F32)
             for u in range(2):
                 nc.tensor.transpose(xT_banks[s][:, i, u, :], x_words[:, u : MUL // 2 : 2], ident_f32[:])
@@ -165,7 +165,7 @@ def tile_loracuetlinear_pa_t_e_kernel(tc, x, a_lora, w_base_words, w_base_scales
             m = STEP * s + i
             g = IRREP_OF_BLOCK[m % BLOCKS]
             nodes = slice(i * P, (i + 1) * P)
-            mx_banks[m] = psum.tile([P, MUL], F32, name="mx_bank")
+            mx_banks[m] = psum.tile([P, MUL], F32, name="mx_bank", bufs=3)
             nc.tensor.matmul_mx(
                 out=mx_banks[m][:],
                 lhsT=code_tiles[s][:, nodes].bitcast(FP8X4),

import math
from contextlib import ExitStack

import concourse.mybir as mybir
from concourse.masks import make_identity

BF16 = mybir.dt.bfloat16
F32 = mybir.dt.float32
I32 = mybir.dt.int32
U8 = mybir.dt.uint8
U32 = mybir.dt.uint32
FP8X4 = mybir.dt.float8_e4m3fn_x4
FP4X4 = mybir.dt.float4_e2m1fn_x4

P = 128
PACK = 4
NODES = 1024
MUL = 512
RANK = 128
IRREP_DIMS = (1, 3, 5)
IRREPS = len(IRREP_DIMS)
IRREP_OF_BLOCK = tuple(k for k, d in enumerate(IRREP_DIMS) for c in range(d))
BLOCKS = len(IRREP_OF_BLOCK)
NODES_PER_PARTITION = NODES // P

PANELS = NODES_PER_PARTITION * BLOCKS
STEP = 2
STEPS = PANELS // STEP
AHEAD = 3
LOAD_ORDER = (
    ("x", 2),
    ("a", 8),
    ("scales", 0),
    ("x", 2),
    ("x", 4),
    ("weights", 0),
    ("a", 8),
    ("x", 4),
    ("weights", 2),
    ("x", 8),
    ("a", 16),
    ("x", 16),
    ("a", 40),
    ("x", 36),
)
WARM_UP = 5
STORES = (8, 8, 8, 8, 8, 8, 8, 6, 4, 3, 2, 1)

BASE_FACTOR = 1.0 / math.sqrt(MUL)
LORA_FACTOR = 2.0 / math.sqrt(RANK)

FLOPS = 2 * NODES * BLOCKS * MUL * (MUL + RANK)


def tile_loracuetlinear_pa_t_e_kernel(tc, x, a_lora, w_base_words, w_base_scales, w_lora_b, out):
    nc = tc.nc
    x_panels = x.rearrange("(p t) c -> p (t c)", p=P).rearrange("p (m k) -> p m k", k=MUL)
    a_panels = a_lora.rearrange("(p t) c -> p (t c)", p=P).rearrange("p (m r) -> p m r", r=RANK)
    out_panels = out.rearrange("(p t) c -> p (t c)", p=P).rearrange("p (m c) -> p m c", c=MUL)

    with ExitStack() as ctx:
        keep = ctx.enter_context(tc.tile_pool(name="keep", bufs=1))
        ring = ctx.enter_context(tc.tile_pool(name="ring", bufs=4))
        results = ctx.enter_context(tc.tile_pool(name="results", bufs=6))
        psum = ctx.enter_context(tc.psum_pool(name="psum", bufs=2))
        ctx.enter_context(tc.manual_schedule())

        ident_f32 = keep.tile([P, P], F32)
        make_identity(nc, ident_f32[:])
        ident_bf16 = keep.tile([P, P], BF16)
        make_identity(nc, ident_bf16[:])

        w_words = keep.tile([P, IRREPS, 2 * MUL], U8, align_bytes=64)
        w_planes = keep.tile([P, IRREPS, MUL], U8, align_bytes=64)
        nc.vector.memset(w_planes[:].bitcast(I32), 0)
        zeros = keep.tile([P, MUL], BF16)
        nc.vector.memset(zeros[:], 0.0)
        w_lora = keep.tile([P, IRREPS, MUL], BF16)

        x_of_panel = {}
        a_of_panel = {}
        for what, count in LOAD_ORDER:
            if what == "x":
                first = len(x_of_panel)
                x_load = keep.tile([P, count, MUL], BF16, name="x_load%d" % first)
                nc.sync.dma_start(out=x_load[:], in_=x_panels[:, first : first + count, :])
                for i in range(count):
                    x_of_panel[first + i] = x_load[:, i, :]
            elif what == "a":
                first = len(a_of_panel)
                a_load = keep.tile([P, count, RANK], BF16, name="a_load%d" % first)
                nc.sync.dma_start(out=a_load[:], in_=a_panels[:, first : first + count, :])
                for i in range(count):
                    a_of_panel[first + i] = a_load[:, i, :]
            elif what == "scales":
                for quadrant in range(4):
                    nc.sync.dma_start(
                        out=w_planes[32 * quadrant : 32 * quadrant + 4, :, :].bitcast(I32),
                        in_=w_base_scales.bitcast(I32)[:, 4 * quadrant : 4 * quadrant + 4, :].rearrange(
                            "g q w -> q g w"
                        ),
                    )
            else:
                irreps = slice(0, 2) if count == 0 else slice(2, IRREPS)
                nc.sync.dma_start(out=w_lora[:, irreps, :], in_=w_lora_b[irreps].rearrange("g r c -> r g c"))
                nc.sync.dma_start(
                    out=w_words[:, irreps, :].bitcast(I32),
                    in_=w_base_words[irreps].bitcast(I32).rearrange("g p w -> p g w"),
                )
        assert len(x_of_panel) == PANELS and len(a_of_panel) == PANELS

        store_starts = [sum(STORES[:g]) for g in range(len(STORES))]
        store_ends = store_starts[1:] + [PANELS]
        assert sum(STORES) == PANELS

        xT_banks = {}
        aT_banks = {}
        grouped_tiles = {}
        aT_tiles = {}
        code_tiles = {}
        plane_tiles = {}
        lora_banks = {}
        mx_banks = {}
        lora_tiles = {}
        out_tiles = {}

        def transpose_panel(s, i):
            m = STEP * s + i
            if i == 0:
                xT_banks[s] = psum.tile([P, STEP, 2, P], F32, name="xT_bank")
                aT_banks[s] = psum.tile([P, STEP, P], BF16, name="aT_bank", bufs=1)
            x_words = x_of_panel[m].bitcast(F32)
            for u in range(2):
                nc.tensor.transpose(xT_banks[s][:, i, u, :], x_words[:, u : MUL // 2 : 2], ident_f32[:])
            nc.tensor.transpose(aT_banks[s][:, i, :], a_of_panel[m], ident_bf16[:])

        def copy_x_out(s):
            grouped = ring.tile([P, STEP, P, PACK], BF16, name="grouped", align_bytes=64)
            nc.scalar.copy(out=grouped[:].bitcast(F32), in_=xT_banks[s][:].rearrange("p i u n -> p i n u"))
            grouped_tiles[s] = grouped

        def copy_a_out(s):
            aT = ring.tile([P, STEP, P], BF16, name="aT")
            nc.vector.tensor_copy(out=aT[:], in_=aT_banks[s][:])
            aT_tiles[s] = aT

        def quantise(s):
            codes = ring.tile([P, STEP * P], U32, name="codes", align_bytes=64)
            planes = ring.tile([P, STEP * P], U8, name="planes", align_bytes=64)
            nc.vector.quantize_mx(
                out=codes[:].bitcast(FP8X4),
                scales=planes[:],
                in_=grouped_tiles[s][:].rearrange("p i n t -> p (i n t)"),
            )
            code_tiles[s] = codes
            plane_tiles[s] = planes

        def lora_product(s, i):
            m = STEP * s + i
            g = IRREP_OF_BLOCK[m % BLOCKS]
            lora_banks[m] = psum.tile([P, MUL], F32, name="lora_bank")
            nc.tensor.matmul(lora_banks[m][:], lhsT=aT_tiles[s][:, i, :], rhs=w_lora[:, g, :], start=True, stop=True)

        def base_product(s, i):
            m = STEP * s + i
            g = IRREP_OF_BLOCK[m % BLOCKS]
            nodes = slice(i * P, (i + 1) * P)
            mx_banks[m] = psum.tile([P, MUL], F32, name="mx_bank", bufs=3)
            nc.tensor.matmul_mx(
                out=mx_banks[m][:],
                lhsT=code_tiles[s][:, nodes].bitcast(FP8X4),
                lhsT_scale=plane_tiles[s][:, nodes],
                rhs=w_words[:, g, :].bitcast(FP4X4),
                rhs_scale=w_planes[:, g, :],
                start=True,
                stop=True,
            )

        def scale_lora(m):
            lora_tiles[m] = ring.tile([P, MUL], F32, name="lora_scaled")
            nc.scalar.activation(
                out=lora_tiles[m][:], in_=lora_banks[m][:], func=mybir.ActivationFunctionType.Copy, scale=LORA_FACTOR
            )

        def combine_and_store(m):
            group = max(g for g in range(len(store_starts)) if store_starts[g] <= m)
            start = store_starts[group]
            end = store_ends[group]
            if m == start:
                out_tiles[group] = results.tile([P, end - start, MUL], F32, name="out_tile")
            nc.vector.scalar_tensor_tensor(
                out=out_tiles[group][:, m - start, :],
                in0=mx_banks[m][:],
                scalar=BASE_FACTOR,
                in1=lora_tiles[m][:],
                op0=mybir.AluOpType.mult,
                op1=mybir.AluOpType.add,
            )
            if m == end - 1:
                nc.sync.dma_start(out=out_panels[:, start:end, :], in_=out_tiles[group][:])

        warm_bank = psum.tile([P, MUL], F32, name="lora_bank")
        for w in range(WARM_UP):
            nc.tensor.matmul(warm_bank[:], lhsT=zeros[:, :P], rhs=zeros[:], start=True, stop=True)
        for s in range(AHEAD):
            for i in range(STEP):
                transpose_panel(s, i)
            copy_x_out(s)
            copy_a_out(s)
        for s in range(AHEAD - 1):
            quantise(s)

        for s in range(STEPS):
            ahead = s + AHEAD
            for i in range(STEP):
                lora_product(s, i)
                if ahead < STEPS:
                    transpose_panel(ahead, i)
            for i in range(STEP):
                base_product(s, i)
            for i in range(STEP):
                scale_lora(STEP * s + i)
            if ahead < STEPS:
                copy_x_out(ahead)
            if ahead - 1 < STEPS:
                quantise(ahead - 1)
            if ahead < STEPS:
                copy_a_out(ahead)
            for i in range(STEP):
                combine_and_store(STEP * s + i)
